import numpy as np
import ml_dtypes


def mxq(x, axis, fmt="e4m3"):
    dtype, down = {"e4m3": (ml_dtypes.float8_e4m3fn, 7), "e5m2": (ml_dtypes.float8_e5m2, 14)}[fmt]
    v = np.moveaxis(np.asarray(x, np.float32).astype(ml_dtypes.bfloat16).astype(np.float64), axis, -1)
    blocks = v.reshape(v.shape[:-1] + (-1, 32))
    amax = np.abs(blocks).max(-1, keepdims=True)
    byte = np.maximum(np.where(amax > 0, np.frexp(amax)[1] - 1 + 127, 0) - down, 1)
    scale = np.exp2(byte - 127.0)
    codes = (blocks / scale).astype(np.float32).astype(dtype).astype(np.float64)
    return np.moveaxis((codes * scale).reshape(v.shape), -1, axis)


WIDE = False


def mx_kscale(k):
    if not WIDE:
        return np.ones(k)
    levels = np.array([10, -10, 5, -5, 0])
    if k % 512:
        return np.exp2(np.random.permutation(np.resize(levels, k // 32))).repeat(32)
    a = np.empty((k // 512, 16))
    for p in range(k // 512):
        a[p, :8] = np.random.permutation(np.resize(levels, 8))
        for g in range(8):
            far = levels[np.abs(levels - a[p, g]) >= 10]
            a[p, g + 8] = far[np.random.randint(len(far))]
    return np.exp2(a.ravel()).repeat(32)


BF16 = ml_dtypes.bfloat16


def bf(x):
    return np.asarray(x, np.float32).astype(BF16)


def f64(x):
    return np.asarray(x).astype(np.float64)


B, CIN, COUT, T, R, C = 2, 512, 512, 8, 8, 8


def setup_inputs():
    s = mx_kscale(CIN)
    x = np.random.standard_normal((B, CIN, T, R, C)) * s[None, :, None, None, None]
    W = np.random.standard_normal((7 * COUT, CIN)) * 0.5 / np.sqrt(CIN) / s[None, :]
    return {"x": bf(x), "W": bf(W)}


def _shift(a, axis, d):
    pads = [(0, 0)] * a.ndim
    idx = [slice(None)] * a.ndim
    if d > 0:
        pads[axis] = (1, 0)
        idx[axis] = slice(0, -1)
    else:
        pads[axis] = (0, 1)
        idx[axis] = slice(1, None)
    return np.pad(a, pads)[tuple(idx)]


def reference(x, W):
    cout = W.shape[0] // 7
    xq = mxq(f64(x), 1, "e4m3")
    Wq = mxq(f64(W), 1, "e4m3")
    all_out = xq.transpose(0, 2, 3, 4, 1) @ Wq.T
    a = all_out.reshape(*all_out.shape[:4], 7, cout)
    out = a[..., 0, :]
    out = out + _shift(a[..., 1, :], 1, +1)
    out = out + _shift(a[..., 2, :], 1, -1)
    out = out + _shift(a[..., 3, :], 2, +1)
    out = out + _shift(a[..., 4, :], 2, -1)
    out = out + _shift(a[..., 5, :], 3, +1)
    out = out + _shift(a[..., 6, :], 3, -1)
    return np.transpose(out, (0, 4, 1, 2, 3))

@@ -1,0 +1,283 @@
+from contextlib import ExitStack
+
+import concourse.bass as bass
+import concourse.mybir as mybir
+import concourse.tile as tile
+from concourse.masks import make_identity
+
+F32 = mybir.dt.float32
+BF16 = mybir.dt.bfloat16
+I32 = mybir.dt.int32
+U32 = mybir.dt.uint32
+U8 = mybir.dt.uint8
+FP8X4 = mybir.dt.float8_e4m3fn_x4
+
+P = 128
+NB = 2
+NDIR = 7
+NM = 4
+VOX = 512
+NOPS = NDIR * NM
+FLOPS = 2 * NB * VOX * NDIR * 512 * 512
+PINNED = True
+
+
+def tile_stackeddirectionalconv3d_kernel(tc, x, W, out):
+    nc = tc.nc
+    with ExitStack() as ctx:
+        keep = ctx.enter_context(tc.tile_pool(name="keep", bufs=1))
+        stage = ctx.enter_context(tc.tile_pool(name="stage", bufs=4))
+        ostage = ctx.enter_context(tc.tile_pool(name="ostage", bufs=5))
+        psum = ctx.enter_context(tc.psum_pool(name="psum", bufs=8))
+        if PINNED:
+            ctx.enter_context(tc.manual_schedule())
+
+        ident = keep.tile([P, P], F32, name="ident")
+        xraw = [keep.tile([P, 4 * VOX], BF16, name="xraw%d" % b) for b in range(NB)]
+        wraw = keep.tile([P, NOPS * 512], BF16, name="wraw")
+        g0 = [keep.tile([P, 4 * VOX], BF16, name="g0_%d" % b, align_bytes=64) for b in range(NB)]
+        gc = [keep.tile([P, 8 * VOX], BF16, name="gc_%d" % b, align_bytes=64) for b in range(NB)]
+        XW = 64 + NB * 576
+        xc = keep.tile([P, XW], U32, name="xc", align_bytes=64)
+        xs = keep.tile([P, XW], U8, name="xs", align_bytes=64)
+        xrc = keep.tile([P, NB * 2 * VOX], U32, name="xrc", align_bytes=64)
+        xrs = keep.tile([P, NB * 2 * VOX], U8, name="xrs", align_bytes=64)
+        xcc = keep.tile([P, NB * 2 * VOX], U32, name="xcc", align_bytes=64)
+        xcs = keep.tile([P, NB * 2 * VOX], U8, name="xcs", align_bytes=64)
+        wc = keep.tile([P, NOPS * P], U32, name="wc", align_bytes=64)
+        ws = keep.tile([P, NOPS * P], U8, name="ws", align_bytes=64)
+        ob0 = keep.tile([P, NM * VOX], F32, name="ob0")
+
+        xcI = xc[:].bitcast(I32)
+        xsI = xs[:].bitcast(I32)
+        xrcI = xrc[:].bitcast(I32)
+        xrsI = xrs[:].bitcast(I32)
+        wrawF = wraw[:].bitcast(F32)
+
+        def load_x(b):
+            nc.sync.dma_start(
+                out=xraw[b][:],
+                in_=x[b].rearrange("(q j) t r c -> q (j t r c)", j=4),
+            )
+
+        wsrc = W.rearrange("(k p m) c -> p k (m c)", k=NDIR, m=NM)
+        wdst = wraw[:].rearrange("p (k f) -> p k f", k=NDIR)
+
+        def load_w(k, f0, f1):
+            nc.sync.dma_start(out=wdst[:, k, f0:f1], in_=wsrc[:, k, f0:f1])
+
+        load_x(0)
+        load_w(0, 0, 1024)
+        load_w(0, 1024, 2048)
+        load_w(1, 0, 1024)
+        load_w(1, 1024, 2048)
+        load_w(2, 0, 2048)
+        load_w(3, 0, 2048)
+        load_w(4, 0, 2048)
+        load_w(5, 0, 2048)
+        load_x(1)
+        load_w(6, 0, 2048)
+
+        zt = keep.tile([P, 512], BF16, name="zt")
+        nc.vector.memset(zt[:].bitcast(I32), 0)
+        make_identity(nc, ident[:])
+        warm = psum.tile([P, 512], F32, name="bank")
+
+        def dummy(n, rhs):
+            for i in range(n):
+                nc.tensor.matmul(out=warm[:], lhsT=zt[:, 0:P], rhs=rhs, start=True, stop=True)
+
+        dummy(6, zt[:])
+        dummy(2, xraw[0][:, 0:512])
+
+        nc.vector.memset(xsI, 0)
+        nc.vector.memset(xcI[:, 0 : NB * 576].rearrange("p (a c) -> p a c", c=576)[:, :, 0:64], 0)
+        nc.vector.memset(xcI[:, NB * 576 : XW], 0)
+        xrc4 = xrcI.rearrange("p (b d t c) -> p b d t c", b=NB, d=2, c=64)
+        xrs4 = xrsI.rearrange("p (b d t c) -> p b d t c", b=NB, d=2, c=16)
+
+        def r_borders():
+            nc.vector.memset(xrc4[:, :, 0, :, 0:8], 0)
+            nc.vector.memset(xrc4[:, :, 1, :, 56:64], 0)
+            nc.vector.memset(xrs4[:, :, 0, :, 0:2], 0)
+            nc.vector.memset(xrs4[:, :, 1, :, 14:16], 0)
+
+        def c_borders(b):
+            gcI = gc[b][:].bitcast(I32).rearrange("p (d r c) -> p d r c", d=2, c=16)
+            nc.vector.memset(gcI[:, 0, :, 0:2], 0)
+            nc.vector.memset(gcI[:, 1, :, 14:16], 0)
+
+        def x_regroup(b, c0, c1):
+            nc.vector.tensor_copy(
+                out=g0[b][:, 4 * c0 : 4 * c1].rearrange("p (c i j) -> p c j i", i=4, j=4),
+                in_=xraw[b][:].rearrange("p (j w) -> p j w", j=4)[:, :, c0:c1].rearrange(
+                    "p j (c i) -> p c j i", i=4
+                ),
+            )
+
+        def x_qself(b, c0, c1):
+            lo = 64 + 576 * b
+            nc.vector.quantize_mx(
+                out=xc[:, lo + c0 : lo + c1].bitcast(FP8X4),
+                scales=xs[:, lo + c0 : lo + c1],
+                in_=g0[b][:, 4 * c0 : 4 * c1],
+            )
+
+        def x_ccopy(b):
+            src = g0[b][:].rearrange("p (r c) -> p r c", c=32)
+            dst = gc[b][:].rearrange("p (d r c) -> p d r c", d=2, c=32)
+            nc.vector.tensor_copy(out=dst[:, 0, :, 4:32], in_=src[:, :, 0:28])
+            nc.vector.tensor_copy(out=dst[:, 1, :, 0:28], in_=src[:, :, 4:32])
+
+        def x_qc(b):
+            lo = 2 * VOX * b
+            nc.vector.quantize_mx(
+                out=xcc[:, lo : lo + 2 * VOX].bitcast(FP8X4), scales=xcs[:, lo : lo + 2 * VOX], in_=gc[b][:]
+            )
+
+        def x_rmove(b):
+            lo = 64 + 576 * b
+            cs = xcI[:, lo : lo + VOX].rearrange("p (t c) -> p t c", c=64)
+            ss = xsI[:, lo // 4 : lo // 4 + VOX // 4].rearrange("p (t c) -> p t c", c=16)
+            nc.vector.tensor_copy(out=xrc4[:, b, 0, :, 8:64], in_=cs[:, :, 0:56])
+            nc.vector.tensor_copy(out=xrs4[:, b, 0, :, 2:16], in_=ss[:, :, 0:14])
+            nc.vector.tensor_copy(out=xrc4[:, b, 1, :, 0:56], in_=cs[:, :, 8:64])
+            nc.vector.tensor_copy(out=xrs4[:, b, 1, :, 0:14], in_=ss[:, :, 2:16])
+
+        def moving(b, k, c0, c1):
+            if k < 3:
+                lo = 576 * b + (64, 0, 128)[k]
+                return xc[:, lo + c0 : lo + c1], xs[:, lo + c0 : lo + c1]
+            lo = 2 * VOX * b + VOX * ((k - 3) % 2)
+            if k < 5:
+                return xrc[:, lo + c0 : lo + c1], xrs[:, lo + c0 : lo + c1]
+            return xcc[:, lo + c0 : lo + c1], xcs[:, lo + c0 : lo + c1]
+
+        banks = {}
+        gws = {}
+
+        def w_transpose(k, h):
+            ps = psum.tile([P, 512], F32, name="bank")
+            banks[(k, h)] = ps
+            for kk in range(2):
+                for u in range(2):
+                    idx = 4 * k + 2 * h + kk
+                    nc.tensor.transpose(
+                        ps[:, 256 * kk + 128 * u : 256 * kk + 128 * u + 128],
+                        wrawF[:, 256 * idx + u : 256 * idx + 256 : 2],
+                        ident[:],
+                    )
+
+        def w_copy(k, h):
+            if h == 0:
+                gw = stage.tile([P, 1024], F32, name="gw", align_bytes=64)
+                gws[k] = gw
+            nc.scalar.copy(
+                out=gws[k][:, 512 * h : 512 * h + 512].rearrange("p (k o u) -> p k o u", k=2, u=2),
+                in_=banks[(k, h)][:].rearrange("p (k u o) -> p k o u", k=2, u=2),
+            )
+
+        def w_quant(k, h0, h1):
+            lo = 512 * k
+            nc.vector.quantize_mx(
+                out=wc[:, lo + 256 * h0 : lo + 256 * h1].bitcast(FP8X4),
+                scales=ws[:, lo + 256 * h0 : lo + 256 * h1],
+                in_=gws[k][:, 512 * h0 : 512 * h1].bitcast(BF16),
+            )
+
+        def mx(acc, m, b, k, c0, c1):
+            idx = 4 * k + m
+            rc, rs = moving(b, k, c0, c1)
+            nc.tensor.matmul_mx(
+                out=acc[:, 0 : c1 - c0],
+                lhsT=wc[:, P * idx : P * idx + P].bitcast(FP8X4),
+                lhsT_scale=ws[:, P * idx : P * idx + P],
+                rhs=rc.bitcast(FP8X4),
+                rhs_scale=rs,
+                start=(k == 0),
+                stop=(k == NDIR - 1),
+            )
+
+        def copy_out(eng, dst, src):
+            if eng == 0:
+                nc.scalar.copy(out=dst, in_=src)
+            else:
+                nc.vector.tensor_copy(out=dst, in_=src)
+
+        x_regroup(0, 0, 256)
+        x_regroup(0, 256, 512)
+        x_qself(0, 0, 256)
+        x_qself(0, 256, 512)
+        for h in range(2):
+            w_transpose(0, h)
+            w_copy(0, h)
+        for h in range(2):
+            dummy(1, xraw[0][:, 0:512])
+            w_transpose(1, h)
+            w_copy(1, h)
+        w_quant(0, 0, 1)
+        w_quant(0, 1, 2)
+        r_borders()
+        x_rmove(0)
+        acc0 = [psum.tile([P, 512], F32, name="bank") for m in range(NM)]
+
+        def direction(k):
+            for m in range(NM):
+                mx(acc0[m], m, 0, k, 0, VOX)
+                if k == NDIR - 1:
+                    copy_out(m % 2, ob0[:, VOX * m : VOX * m + VOX], acc0[m][:])
+
+        def w_run(k):
+            for h in range(2):
+                w_transpose(k, h)
+                w_copy(k, h)
+
+        direction(0)
+        w_quant(1, 0, 2)
+        w_run(2)
+        w_run(3)
+        c_borders(0)
+        x_ccopy(0)
+        direction(1)
+        w_quant(2, 0, 2)
+        x_qc(0)
+        w_run(4)
+        w_run(5)
+        w_quant(3, 0, 2)
+        direction(2)
+        direction(3)
+        w_quant(4, 0, 2)
+        x_regroup(1, 0, 512)
+        w_quant(5, 0, 2)
+        w_run(6)
+        x_qself(1, 0, 512)
+        x_rmove(1)
+        w_quant(6, 0, 2)
+        direction(4)
+        c_borders(1)
+        x_ccopy(1)
+        direction(5)
+        x_qc(1)
+        direction(6)
+        nc.sync.dma_start(out=out[0].rearrange("(p m) t r c -> p (m t r c)", m=NM), in_=ob0[:])
+
+        out1 = out[1].rearrange("(p m) t r c -> p m (t r c)", m=NM)
+
+        def finish(acc, m, c0, c1, eng):
+            ob = ostage.tile([P, c1 - c0], F32, name="ob")
+            copy_out(eng, ob[:], acc[:, 0 : c1 - c0])
+            nc.sync.dma_start(out=out1[:, m, c0:c1], in_=ob[:])
+
+        acc1 = [psum.tile([P, 512], F32, name="bank") for m in range(2)]
+        for m in range(2):
+            for k in range(5):
+                mx(acc1[m], m, 1, k, 0, VOX)
+        for m in range(2):
+            for k in range(5, NDIR):
+                mx(acc1[m], m, 1, k, 0, VOX)
+            finish(acc1[m], m, 0, VOX, (m + 1) % 2)
+        for n, (m, c0, c1) in enumerate([(2, 0, VOX), (3, 0, VOX // 2), (3, VOX // 2, VOX)]):
+            acc = psum.tile([P, 512], F32, name="bank")
+            for k in range(NDIR):
+                mx(acc, m, 1, k, c0, c1)
+            finish(acc, m, c0, c1, (n + 1) % 2)

@@ -28,7 +28,7 @@ def tile_stackeddirectionalconv3d_kernel(tc, x, W, out):
         keep = ctx.enter_context(tc.tile_pool(name="keep", bufs=1))
         stage = ctx.enter_context(tc.tile_pool(name="stage", bufs=4))
         ostage = ctx.enter_context(tc.tile_pool(name="ostage", bufs=5))
-        psum = ctx.enter_context(tc.psum_pool(name="psum", bufs=8))
+        psum = ctx.enter_context(tc.psum_pool(name="psum", bufs=1))
         if PINNED:
             ctx.enter_context(tc.manual_schedule())
 
@@ -81,14 +81,18 @@ def tile_stackeddirectionalconv3d_kernel(tc, x, W, out):
         zt = keep.tile([P, 512], BF16, name="zt")
         nc.vector.memset(zt[:].bitcast(I32), 0)
         make_identity(nc, ident[:])
-        warm = psum.tile([P, 512], F32, name="bank")
+
+        def bank(i):
+            t = psum.tile([P, 512], F32, name="bank%d" % i)
+            return t
+
+        warm = bank(3)
 
         def dummy(n, rhs):
             for i in range(n):
                 nc.tensor.matmul(out=warm[:], lhsT=zt[:, 0:P], rhs=rhs, start=True, stop=True)
 
-        dummy(6, zt[:])
-        dummy(2, xraw[0][:, 0:512])
+        dummy(5, zt[:])
 
         nc.vector.memset(xsI, 0)
         nc.vector.memset(xcI[:, 0 : NB * 576].rearrange("p (a c) -> p a c", c=576)[:, :, 0:64], 0)
@@ -157,7 +161,7 @@ def tile_stackeddirectionalconv3d_kernel(tc, x, W, out):
         gws = {}
 
         def w_transpose(k, h):
-            ps = psum.tile([P, 512], F32, name="bank")
+            ps = bank(4 + 2 * (k % 2) + h)
             banks[(k, h)] = ps
             for kk in range(2):
                 for u in range(2):
@@ -204,22 +208,23 @@ def tile_stackeddirectionalconv3d_kernel(tc, x, W, out):
             else:
                 nc.vector.tensor_copy(out=dst, in_=src)
 
+        def w_run(k):
+            for h in range(2):
+                w_transpose(k, h)
+                w_copy(k, h)
+
         x_regroup(0, 0, 256)
         x_regroup(0, 256, 512)
         x_qself(0, 0, 256)
         x_qself(0, 256, 512)
-        for h in range(2):
-            w_transpose(0, h)
-            w_copy(0, h)
-        for h in range(2):
-            dummy(1, xraw[0][:, 0:512])
-            w_transpose(1, h)
-            w_copy(1, h)
+        w_run(0)
+        dummy(2, zt[:])
+        w_run(1)
         w_quant(0, 0, 1)
         w_quant(0, 1, 2)
         r_borders()
         x_rmove(0)
-        acc0 = [psum.tile([P, 512], F32, name="bank") for m in range(NM)]
+        acc0 = [bank(m) for m in range(NM)]
 
         def direction(k):
             for m in range(NM):
@@ -227,37 +232,35 @@ def tile_stackeddirectionalconv3d_kernel(tc, x, W, out):
                 if k == NDIR - 1:
                     copy_out(m % 2, ob0[:, VOX * m : VOX * m + VOX], acc0[m][:])
 
-        def w_run(k):
-            for h in range(2):
-                w_transpose(k, h)
-                w_copy(k, h)
-
         direction(0)
         w_quant(1, 0, 2)
         w_run(2)
-        w_run(3)
         c_borders(0)
         x_ccopy(0)
         direction(1)
         w_quant(2, 0, 2)
+        w_run(3)
         x_qc(0)
-        w_run(4)
-        w_run(5)
-        w_quant(3, 0, 2)
         direction(2)
-        direction(3)
-        w_quant(4, 0, 2)
+        w_quant(3, 0, 2)
+        w_run(4)
         x_regroup(1, 0, 512)
-        w_quant(5, 0, 2)
-        w_run(6)
-        x_qself(1, 0, 512)
-        x_rmove(1)
-        w_quant(6, 0, 2)
-        direction(4)
         c_borders(1)
         x_ccopy(1)
-        direction(5)
+        direction(3)
+        w_quant(4, 0, 2)
+        x_qself(1, 0, 512)
         x_qc(1)
+        w_run(5)
+        direction(4)
+        w_quant(5, 0, 2)
+        x_rmove(1)
+        w_run(6)
+        direction(5)
+        acc1 = [bank(6 + m) for m in range(2)]
+        for m in range(2):
+            mx(acc1[m], m, 1, 0, 0, VOX)
+        w_quant(6, 0, 2)
         direction(6)
         nc.sync.dma_start(out=out[0].rearrange("(p m) t r c -> p (m t r c)", m=NM), in_=ob0[:])
 
@@ -268,16 +271,15 @@ def tile_stackeddirectionalconv3d_kernel(tc, x, W, out):
             copy_out(eng, ob[:], acc[:, 0 : c1 - c0])
             nc.sync.dma_start(out=out1[:, m, c0:c1], in_=ob[:])
 
-        acc1 = [psum.tile([P, 512], F32, name="bank") for m in range(2)]
         for m in range(2):
-            for k in range(5):
+            for k in range(1, 5):
                 mx(acc1[m], m, 1, k, 0, VOX)
         for m in range(2):
             for k in range(5, NDIR):
                 mx(acc1[m], m, 1, k, 0, VOX)
             finish(acc1[m], m, 0, VOX, (m + 1) % 2)
-        for n, (m, c0, c1) in enumerate([(2, 0, VOX), (3, 0, VOX // 2), (3, VOX // 2, VOX)]):
-            acc = psum.tile([P, 512], F32, name="bank")
+        for n, (i, m, c0, c1) in enumerate([(4, 2, 0, VOX), (5, 3, 0, VOX // 2), (0, 3, VOX // 2, VOX)]):
+            acc = bank(i)
             for k in range(NDIR):
                 mx(acc, m, 1, k, c0, c1)
             finish(acc, m, c0, c1, (n + 1) % 2)

@@ -92,7 +92,8 @@ def tile_stackeddirectionalconv3d_kernel(tc, x, W, out):
             for i in range(n):
                 nc.tensor.matmul(out=warm[:], lhsT=zt[:, 0:P], rhs=rhs, start=True, stop=True)
 
-        dummy(5, zt[:])
+        dummy(6, zt[:])
+        dummy(2, xraw[0][:, 0:512])
 
         nc.vector.memset(xsI, 0)
         nc.vector.memset(xcI[:, 0 : NB * 576].rearrange("p (a c) -> p a c", c=576)[:, :, 0:64], 0)
@@ -208,6 +209,10 @@ def tile_stackeddirectionalconv3d_kernel(tc, x, W, out):
             else:
                 nc.vector.tensor_copy(out=dst, in_=src)
 
+        r_borders()
+        c_borders(0)
+        c_borders(1)
+
         def w_run(k):
             for h in range(2):
                 w_transpose(k, h)
@@ -218,11 +223,12 @@ def tile_stackeddirectionalconv3d_kernel(tc, x, W, out):
         x_qself(0, 0, 256)
         x_qself(0, 256, 512)
         w_run(0)
-        dummy(2, zt[:])
-        w_run(1)
+        for h in range(2):
+            dummy(1, xraw[0][:, 0:512])
+            w_transpose(1, h)
+            w_copy(1, h)
         w_quant(0, 0, 1)
         w_quant(0, 1, 2)
-        r_borders()
         x_rmove(0)
         acc0 = [bank(m) for m in range(NM)]
 
@@ -234,23 +240,19 @@ def tile_stackeddirectionalconv3d_kernel(tc, x, W, out):
 
         direction(0)
         w_quant(1, 0, 2)
-        w_run(2)
-        c_borders(0)
         x_ccopy(0)
+        w_run(2)
         direction(1)
         w_quant(2, 0, 2)
-        w_run(3)
         x_qc(0)
+        w_run(3)
         direction(2)
         w_quant(3, 0, 2)
-        w_run(4)
         x_regroup(1, 0, 512)
-        c_borders(1)
-        x_ccopy(1)
+        w_run(4)
         direction(3)
         w_quant(4, 0, 2)
         x_qself(1, 0, 512)
-        x_qc(1)
         w_run(5)
         direction(4)
         w_quant(5, 0, 2)
@@ -259,8 +261,11 @@ def tile_stackeddirectionalconv3d_kernel(tc, x, W, out):
         direction(5)
         acc1 = [bank(6 + m) for m in range(2)]
         for m in range(2):
-            mx(acc1[m], m, 1, 0, 0, VOX)
+            for k in range(3):
+                mx(acc1[m], m, 1, k, 0, VOX)
         w_quant(6, 0, 2)
+        x_ccopy(1)
+        x_qc(1)
         direction(6)
         nc.sync.dma_start(out=out[0].rearrange("(p m) t r c -> p (m t r c)", m=NM), in_=ob0[:])
 
@@ -272,7 +277,7 @@ def tile_stackeddirectionalconv3d_kernel(tc, x, W, out):
             nc.sync.dma_start(out=out1[:, m, c0:c1], in_=ob[:])
 
         for m in range(2):
-            for k in range(1, 5):
+            for k in range(3, 5):
                 mx(acc1[m], m, 1, k, 0, VOX)
         for m in range(2):
             for k in range(5, NDIR):

@@ -18,6 +18,8 @@ NDIR = 7
 NM = 4
 VOX = 512
 NOPS = NDIR * NM
+VDIR = (6,)
+NPE = NDIR - len(VDIR)
 FLOPS = 2 * NB * VOX * NDIR * 512 * 512
 PINNED = True
 
@@ -27,14 +29,17 @@ def tile_stackeddirectionalconv3d_kernel(tc, x, W, out):
     with ExitStack() as ctx:
         keep = ctx.enter_context(tc.tile_pool(name="keep", bufs=1))
         stage = ctx.enter_context(tc.tile_pool(name="stage", bufs=4))
-        ostage = ctx.enter_context(tc.tile_pool(name="ostage", bufs=5))
+        ostage = ctx.enter_context(tc.tile_pool(name="ostage", bufs=9))
         psum = ctx.enter_context(tc.psum_pool(name="psum", bufs=1))
         if PINNED:
             ctx.enter_context(tc.manual_schedule())
 
         ident = keep.tile([P, P], F32, name="ident")
         xraw = [keep.tile([P, 4 * VOX], BF16, name="xraw%d" % b) for b in range(NB)]
-        wraw = keep.tile([P, NOPS * 512], BF16, name="wraw")
+        wraw = keep.tile([P, NPE * 2048], BF16, name="wraw")
+        vraw = [keep.tile([P, 2048], BF16, name="vraw%d" % i) for i in range(len(VDIR))]
+        vin = [keep.tile([P, 1024], F32, name="vin%d" % i, align_bytes=64) for i in range(len(VDIR))]
+        vout = [keep.tile([P, 1024], F32, name="vout%d" % i, align_bytes=64) for i in range(len(VDIR))]
         g0 = [keep.tile([P, 4 * VOX], BF16, name="g0_%d" % b, align_bytes=64) for b in range(NB)]
         gc = [keep.tile([P, 8 * VOX], BF16, name="gc_%d" % b, align_bytes=64) for b in range(NB)]
         XW = 64 + NB * 576
@@ -46,7 +51,6 @@ def tile_stackeddirectionalconv3d_kernel(tc, x, W, out):
         xcs = keep.tile([P, NB * 2 * VOX], U8, name="xcs", align_bytes=64)
         wc = keep.tile([P, NOPS * P], U32, name="wc", align_bytes=64)
         ws = keep.tile([P, NOPS * P], U8, name="ws", align_bytes=64)
-        ob0 = keep.tile([P, NM * VOX], F32, name="ob0")
 
         xcI = xc[:].bitcast(I32)
         xsI = xs[:].bitcast(I32)
@@ -61,10 +65,18 @@ def tile_stackeddirectionalconv3d_kernel(tc, x, W, out):
             )
 
         wsrc = W.rearrange("(k p m) c -> p k (m c)", k=NDIR, m=NM)
-        wdst = wraw[:].rearrange("p (k f) -> p k f", k=NDIR)
+        wdst = wraw[:].rearrange("p (k f) -> p k f", k=NPE)
 
         def load_w(k, f0, f1):
             nc.sync.dma_start(out=wdst[:, k, f0:f1], in_=wsrc[:, k, f0:f1])
+
+        def load_v(k):
+            t = vraw[VDIR.index(k)]
+            for a in (0, 2, 1, 3):
+                nc.sync.dma_start(
+                    out=t[32 * a : 32 * a + 32, :].rearrange("j (x f) -> j x f", f=128),
+                    in_=W[512 * k : 512 * k + 512, 128 * a : 128 * a + 128].rearrange("(x j) f -> j x f", j=32),
+                )
 
         load_x(0)
         load_w(0, 0, 1024)
@@ -76,7 +88,7 @@ def tile_stackeddirectionalconv3d_kernel(tc, x, W, out):
         load_w(4, 0, 2048)
         load_w(5, 0, 2048)
         load_x(1)
-        load_w(6, 0, 2048)
+        load_v(6)
 
         zt = keep.tile([P, 512], BF16, name="zt")
         nc.vector.memset(zt[:].bitcast(I32), 0)
@@ -182,6 +194,23 @@ def tile_stackeddirectionalconv3d_kernel(tc, x, W, out):
                 in_=banks[(k, h)][:].rearrange("p (k u o) -> p k o u", k=2, u=2),
             )
 
+        def v_pick(k):
+            i = VDIR.index(k)
+            nc.scalar.copy(
+                out=vin[i][:].rearrange("p (x h i) -> p x h i", x=16, h=2),
+                in_=vraw[i][:].bitcast(F32).rearrange("p (x i h) -> p x h i", x=16, h=2),
+            )
+
+        def v_transpose(k):
+            i = VDIR.index(k)
+            nc.vector.transpose(out=vout[i][:], in_=vin[i][:])
+
+        def v_copy(k):
+            gw = stage.tile([P, 1024], F32, name="gw", align_bytes=64)
+            gws[k] = gw
+            v = vout[VDIR.index(k)][:].rearrange("p (x h j m) -> p m x j h", x=16, h=2, m=NM)
+            nc.scalar.copy(out=gw[:].rearrange("p (m x j h) -> p m x j h", m=NM, x=16, h=2), in_=v)
+
         def w_quant(k, h0, h1):
             lo = 512 * k
             nc.vector.quantize_mx(
@@ -236,7 +265,14 @@ def tile_stackeddirectionalconv3d_kernel(tc, x, W, out):
             for m in range(NM):
                 mx(acc0[m], m, 0, k, 0, VOX)
                 if k == NDIR - 1:
-                    copy_out(m % 2, ob0[:, VOX * m : VOX * m + VOX], acc0[m][:])
+                    finish(acc0[m], 0, m, 0, VOX, m % 2)
+
+        outs = [out[b].rearrange("(p m) t r c -> p m (t r c)", m=NM) for b in range(NB)]
+
+        def finish(acc, b, m, c0, c1, eng):
+            ob = ostage.tile([P, c1 - c0], F32, name="ob")
+            copy_out(eng, ob[:], acc[:, 0 : c1 - c0])
+            nc.sync.dma_start(out=outs[b][:, m, c0:c1], in_=ob[:])
 
         direction(0)
         w_quant(1, 0, 2)
@@ -244,47 +280,45 @@ def tile_stackeddirectionalconv3d_kernel(tc, x, W, out):
         w_run(2)
         direction(1)
         w_quant(2, 0, 2)
-        x_qc(0)
+        x_regroup(1, 0, 512)
         w_run(3)
         direction(2)
         w_quant(3, 0, 2)
-        x_regroup(1, 0, 512)
+        x_qself(1, 0, 512)
         w_run(4)
         direction(3)
+        v_pick(6)
         w_quant(4, 0, 2)
-        x_qself(1, 0, 512)
+        x_qc(0)
         w_run(5)
+        v_transpose(6)
         direction(4)
+        v_copy(6)
         w_quant(5, 0, 2)
         x_rmove(1)
-        w_run(6)
+
+        acc1 = [bank(4 + m) for m in range(3)]
+
+        def ahead(m, k0, k1):
+            for k in range(k0, k1):
+                mx(acc1[m], m, 1, k, 0, VOX)
+
+        ahead(0, 0, 3)
+        ahead(1, 0, 3)
         direction(5)
-        acc1 = [bank(6 + m) for m in range(2)]
-        for m in range(2):
-            for k in range(3):
-                mx(acc1[m], m, 1, k, 0, VOX)
-        w_quant(6, 0, 2)
         x_ccopy(1)
+        w_quant(6, 0, 2)
         x_qc(1)
+        for m in range(2):
+            ahead(m, 3, 5)
+        ahead(2, 0, 5)
         direction(6)
-        nc.sync.dma_start(out=out[0].rearrange("(p m) t r c -> p (m t r c)", m=NM), in_=ob0[:])
 
-        out1 = out[1].rearrange("(p m) t r c -> p m (t r c)", m=NM)
-
-        def finish(acc, m, c0, c1, eng):
-            ob = ostage.tile([P, c1 - c0], F32, name="ob")
-            copy_out(eng, ob[:], acc[:, 0 : c1 - c0])
-            nc.sync.dma_start(out=out1[:, m, c0:c1], in_=ob[:])
-
-        for m in range(2):
-            for k in range(3, 5):
-                mx(acc1[m], m, 1, k, 0, VOX)
-        for m in range(2):
-            for k in range(5, NDIR):
-                mx(acc1[m], m, 1, k, 0, VOX)
-            finish(acc1[m], m, 0, VOX, (m + 1) % 2)
-        for n, (i, m, c0, c1) in enumerate([(4, 2, 0, VOX), (5, 3, 0, VOX // 2), (0, 3, VOX // 2, VOX)]):
+        for m in range(3):
+            ahead(m, 5, NDIR)
+            finish(acc1[m], 1, m, 0, VOX, (m + 1) % 2)
+        for n, (i, c0, c1) in enumerate([(7, 0, VOX // 2), (0, VOX // 2, VOX)]):
             acc = bank(i)
             for k in range(NDIR):
-                mx(acc, m, 1, k, c0, c1)
-            finish(acc, m, c0, c1, (n + 1) % 2)
+                mx(acc, 3, 1, k, c0, c1)
+            finish(acc, 1, 3, c0, c1, n % 2)

@@ -19,6 +19,7 @@ NM = 4
 VOX = 512
 NOPS = NDIR * NM
 VDIR = (6,)
+SDIR = 5
 NPE = NDIR - len(VDIR)
 FLOPS = 2 * NB * VOX * NDIR * 512 * 512
 PINNED = True
@@ -37,6 +38,7 @@ def tile_stackeddirectionalconv3d_kernel(tc, x, W, out):
         ident = keep.tile([P, P], F32, name="ident")
         xraw = [keep.tile([P, 4 * VOX], BF16, name="xraw%d" % b) for b in range(NB)]
         wraw = keep.tile([P, NPE * 2048], BF16, name="wraw")
+        wpm = keep.tile([P, 1024], F32, name="wpm")
         vraw = [keep.tile([P, 2048], BF16, name="vraw%d" % i) for i in range(len(VDIR))]
         vin = [keep.tile([P, 1024], F32, name="vin%d" % i, align_bytes=64) for i in range(len(VDIR))]
         vout = [keep.tile([P, 1024], F32, name="vout%d" % i, align_bytes=64) for i in range(len(VDIR))]
@@ -70,10 +72,10 @@ def tile_stackeddirectionalconv3d_kernel(tc, x, W, out):
         def load_w(k, f0, f1):
             nc.sync.dma_start(out=wdst[:, k, f0:f1], in_=wsrc[:, k, f0:f1])
 
-        def load_v(k):
+        def load_v(k, eng, quads):
             t = vraw[VDIR.index(k)]
-            for a in (0, 2, 1, 3):
-                nc.sync.dma_start(
+            for a in quads:
+                eng.dma_start(
                     out=t[32 * a : 32 * a + 32, :].rearrange("j (x f) -> j x f", f=128),
                     in_=W[512 * k : 512 * k + 512, 128 * a : 128 * a + 128].rearrange("(x j) f -> j x f", j=32),
                 )
@@ -85,13 +87,14 @@ def tile_stackeddirectionalconv3d_kernel(tc, x, W, out):
         load_w(1, 1024, 2048)
         load_w(2, 0, 2048)
         load_w(3, 0, 2048)
+        load_x(1)
         load_w(4, 0, 2048)
         load_w(5, 0, 2048)
-        load_x(1)
-        load_v(6)
+        load_v(6, nc.sync, (0, 1))
 
-        zt = keep.tile([P, 512], BF16, name="zt")
+        zt = keep.tile([P, P], BF16, name="zt")
         nc.vector.memset(zt[:].bitcast(I32), 0)
+        zrow = zt[:].unsqueeze(1).to_broadcast([P, 4, P])
         make_identity(nc, ident[:])
 
         def bank(i):
@@ -104,7 +107,7 @@ def tile_stackeddirectionalconv3d_kernel(tc, x, W, out):
             for i in range(n):
                 nc.tensor.matmul(out=warm[:], lhsT=zt[:, 0:P], rhs=rhs, start=True, stop=True)
 
-        dummy(6, zt[:])
+        dummy(6, zrow)
         dummy(2, xraw[0][:, 0:512])
 
         nc.vector.memset(xsI, 0)
@@ -140,11 +143,11 @@ def tile_stackeddirectionalconv3d_kernel(tc, x, W, out):
                 in_=g0[b][:, 4 * c0 : 4 * c1],
             )
 
-        def x_ccopy(b):
+        def x_ccopy(b, second):
             src = g0[b][:].rearrange("p (r c) -> p r c", c=32)
             dst = gc[b][:].rearrange("p (d r c) -> p d r c", d=2, c=32)
             nc.vector.tensor_copy(out=dst[:, 0, :, 4:32], in_=src[:, :, 0:28])
-            nc.vector.tensor_copy(out=dst[:, 1, :, 0:28], in_=src[:, :, 4:32])
+            second(out=dst[:, 1, :, 0:28], in_=src[:, :, 4:32])
 
         def x_qc(b):
             lo = 2 * VOX * b
@@ -178,12 +181,18 @@ def tile_stackeddirectionalconv3d_kernel(tc, x, W, out):
             banks[(k, h)] = ps
             for kk in range(2):
                 for u in range(2):
-                    idx = 4 * k + 2 * h + kk
-                    nc.tensor.transpose(
-                        ps[:, 256 * kk + 128 * u : 256 * kk + 128 * u + 128],
-                        wrawF[:, 256 * idx + u : 256 * idx + 256 : 2],
-                        ident[:],
-                    )
+                    at = 256 * (2 * h + kk)
+                    if k == SDIR:
+                        words = wpm[:, at + 128 * u : at + 128 * u + 128]
+                    else:
+                        words = wrawF[:, 1024 * k + at + u : 1024 * k + at + 256 : 2]
+                    nc.tensor.transpose(ps[:, 256 * kk + 128 * u : 256 * kk + 128 * u + 128], words, ident[:])
+
+        def s_reorder():
+            nc.scalar.copy(
+                out=wpm[:].rearrange("p (m u q) -> p m u q", m=NM, u=2),
+                in_=wrawF[:, 1024 * SDIR : 1024 * SDIR + 1024].rearrange("p (m q u) -> p m u q", m=NM, u=2),
+            )
 
         def w_copy(k, h):
             if h == 0:
@@ -208,8 +217,10 @@ def tile_stackeddirectionalconv3d_kernel(tc, x, W, out):
         def v_copy(k):
             gw = stage.tile([P, 1024], F32, name="gw", align_bytes=64)
             gws[k] = gw
+            dst = gw[:].rearrange("p (m x j h) -> p m x j h", m=NM, x=16, h=2)
             v = vout[VDIR.index(k)][:].rearrange("p (x h j m) -> p m x j h", x=16, h=2, m=NM)
-            nc.scalar.copy(out=gw[:].rearrange("p (m x j h) -> p m x j h", m=NM, x=16, h=2), in_=v)
+            nc.scalar.copy(out=dst[:, 0:2], in_=v[:, 0:2])
+            nc.vector.tensor_copy(out=dst[:, 2:4], in_=v[:, 2:4])
 
         def w_quant(k, h0, h1):
             lo = 512 * k
@@ -276,8 +287,9 @@ def tile_stackeddirectionalconv3d_kernel(tc, x, W, out):
 
         direction(0)
         w_quant(1, 0, 2)
-        x_ccopy(0)
+        x_ccopy(0, nc.vector.tensor_copy)
         w_run(2)
+        load_v(6, nc.scalar, (2, 3))
         direction(1)
         w_quant(2, 0, 2)
         x_regroup(1, 0, 512)
@@ -286,16 +298,10 @@ def tile_stackeddirectionalconv3d_kernel(tc, x, W, out):
         w_quant(3, 0, 2)
         x_qself(1, 0, 512)
         w_run(4)
+        s_reorder()
         direction(3)
-        v_pick(6)
         w_quant(4, 0, 2)
         x_qc(0)
-        w_run(5)
-        v_transpose(6)
-        direction(4)
-        v_copy(6)
-        w_quant(5, 0, 2)
-        x_rmove(1)
 
         acc1 = [bank(4 + m) for m in range(3)]
 
@@ -305,12 +311,19 @@ def tile_stackeddirectionalconv3d_kernel(tc, x, W, out):
 
         ahead(0, 0, 3)
         ahead(1, 0, 3)
+        v_pick(6)
+        w_run(5)
+        x_rmove(1)
+        v_transpose(6)
+        direction(4)
+        ahead(0, 3, 5)
+        ahead(1, 3, 5)
+        w_quant(5, 0, 2)
         direction(5)
-        x_ccopy(1)
+        v_copy(6)
         w_quant(6, 0, 2)
+        x_ccopy(1, nc.scalar.copy)
         x_qc(1)
-        for m in range(2):
-            ahead(m, 3, 5)
         ahead(2, 0, 5)
         direction(6)
 

from contextlib import ExitStack

import concourse.bass as bass
import concourse.mybir as mybir
import concourse.tile as tile
from concourse.masks import make_identity

F32 = mybir.dt.float32
BF16 = mybir.dt.bfloat16
I32 = mybir.dt.int32
U32 = mybir.dt.uint32
U8 = mybir.dt.uint8
FP8X4 = mybir.dt.float8_e4m3fn_x4

P = 128
NB = 2
NDIR = 7
NM = 4
VOX = 512
NOPS = NDIR * NM
VDIR = (6,)
SDIR = 5
NPE = NDIR - len(VDIR)
FLOPS = 2 * NB * VOX * NDIR * 512 * 512
PINNED = True


def tile_stackeddirectionalconv3d_kernel(tc, x, W, out):
    nc = tc.nc
    with ExitStack() as ctx:
        keep = ctx.enter_context(tc.tile_pool(name="keep", bufs=1))
        stage = ctx.enter_context(tc.tile_pool(name="stage", bufs=4))
        ostage = ctx.enter_context(tc.tile_pool(name="ostage", bufs=9))
        psum = ctx.enter_context(tc.psum_pool(name="psum", bufs=1))
        if PINNED:
            ctx.enter_context(tc.manual_schedule())

        ident = keep.tile([P, P], F32, name="ident")
        xraw = [keep.tile([P, 4 * VOX], BF16, name="xraw%d" % b) for b in range(NB)]
        wraw = keep.tile([P, NPE * 2048], BF16, name="wraw")
        wpm = keep.tile([P, 1024], F32, name="wpm")
        vraw = [keep.tile([P, 2048], BF16, name="vraw%d" % i) for i in range(len(VDIR))]
        vin = [keep.tile([P, 1024], F32, name="vin%d" % i, align_bytes=64) for i in range(len(VDIR))]
        vout = [keep.tile([P, 1024], F32, name="vout%d" % i, align_bytes=64) for i in range(len(VDIR))]
        g0 = [keep.tile([P, 4 * VOX], BF16, name="g0_%d" % b, align_bytes=64) for b in range(NB)]
        gc = [keep.tile([P, 8 * VOX], BF16, name="gc_%d" % b, align_bytes=64) for b in range(NB)]
        XW = 64 + NB * 576
        xc = keep.tile([P, XW], U32, name="xc", align_bytes=64)
        xs = keep.tile([P, XW], U8, name="xs", align_bytes=64)
        xrc = keep.tile([P, NB * 2 * VOX], U32, name="xrc", align_bytes=64)
        xrs = keep.tile([P, NB * 2 * VOX], U8, name="xrs", align_bytes=64)
        xcc = keep.tile([P, NB * 2 * VOX], U32, name="xcc", align_bytes=64)
        xcs = keep.tile([P, NB * 2 * VOX], U8, name="xcs", align_bytes=64)
        wc = keep.tile([P, NOPS * P], U32, name="wc", align_bytes=64)
        ws = keep.tile([P, NOPS * P], U8, name="ws", align_bytes=64)

        xcI = xc[:].bitcast(I32)
        xsI = xs[:].bitcast(I32)
        xrcI = xrc[:].bitcast(I32)
        xrsI = xrs[:].bitcast(I32)
        wrawF = wraw[:].bitcast(F32)

        def load_x(b):
            nc.sync.dma_start(
                out=xraw[b][:],
                in_=x[b].rearrange("(q j) t r c -> q (j t r c)", j=4),
            )

        wsrc = W.rearrange("(k p m) c -> p k (m c)", k=NDIR, m=NM)
        wdst = wraw[:].rearrange("p (k f) -> p k f", k=NPE)

        def load_w(k, f0, f1):
            nc.sync.dma_start(out=wdst[:, k, f0:f1], in_=wsrc[:, k, f0:f1])

        def load_v(k, eng, quads):
            t = vraw[VDIR.index(k)]
            for a in quads:
                eng.dma_start(
                    out=t[32 * a : 32 * a + 32, :].rearrange("j (x f) -> j x f", f=128),
                    in_=W[512 * k : 512 * k + 512, 128 * a : 128 * a + 128].rearrange("(x j) f -> j x f", j=32),
                )

        load_x(0)
        load_w(0, 0, 1024)
        load_w(0, 1024, 2048)
        load_w(1, 0, 1024)
        load_w(1, 1024, 2048)
        load_w(2, 0, 2048)
        load_w(3, 0, 2048)
        load_x(1)
        load_w(4, 0, 2048)
        load_w(5, 0, 2048)
        load_v(6, nc.sync, (0, 1))

        zt = keep.tile([P, P], BF16, name="zt")
        nc.vector.memset(zt[:].bitcast(I32), 0)
        zrow = zt[:].unsqueeze(1).to_broadcast([P, 4, P])
        make_identity(nc, ident[:])

        def bank(i):
            t = psum.tile([P, 512], F32, name="bank%d" % i)
            return t

        warm = bank(3)

        def dummy(n, rhs):
            for i in range(n):
                nc.tensor.matmul(out=warm[:], lhsT=zt[:, 0:P], rhs=rhs, start=True, stop=True)

        dummy(6, zrow)
        dummy(2, xraw[0][:, 0:512])

        nc.vector.memset(xsI, 0)
        nc.vector.memset(xcI[:, 0 : NB * 576].rearrange("p (a c) -> p a c", c=576)[:, :, 0:64], 0)
        nc.vector.memset(xcI[:, NB * 576 : XW], 0)
        xrc4 = xrcI.rearrange("p (b d t c) -> p b d t c", b=NB, d=2, c=64)
        xrs4 = xrsI.rearrange("p (b d t c) -> p b d t c", b=NB, d=2, c=16)

        def r_borders():
            nc.vector.memset(xrc4[:, :, 0, :, 0:8], 0)
            nc.vector.memset(xrc4[:, :, 1, :, 56:64], 0)
            nc.vector.memset(xrs4[:, :, 0, :, 0:2], 0)
            nc.vector.memset(xrs4[:, :, 1, :, 14:16], 0)

        def c_borders(b):
            gcI = gc[b][:].bitcast(I32).rearrange("p (d r c) -> p d r c", d=2, c=16)
            nc.vector.memset(gcI[:, 0, :, 0:2], 0)
            nc.vector.memset(gcI[:, 1, :, 14:16], 0)

        def x_regroup(b, c0, c1):
            nc.vector.tensor_copy(
                out=g0[b][:, 4 * c0 : 4 * c1].rearrange("p (c i j) -> p c j i", i=4, j=4),
                in_=xraw[b][:].rearrange("p (j w) -> p j w", j=4)[:, :, c0:c1].rearrange(
                    "p j (c i) -> p c j i", i=4
                ),
            )

        def x_qself(b, c0, c1):
            lo = 64 + 576 * b
            nc.vector.quantize_mx(
                out=xc[:, lo + c0 : lo + c1].bitcast(FP8X4),
                scales=xs[:, lo + c0 : lo + c1],
                in_=g0[b][:, 4 * c0 : 4 * c1],
            )

        def x_ccopy(b, second):
            src = g0[b][:].rearrange("p (r c) -> p r c", c=32)
            dst = gc[b][:].rearrange("p (d r c) -> p d r c", d=2, c=32)
            nc.vector.tensor_copy(out=dst[:, 0, :, 4:32], in_=src[:, :, 0:28])
            second(out=dst[:, 1, :, 0:28], in_=src[:, :, 4:32])

        def x_qc(b):
            lo = 2 * VOX * b
            nc.vector.quantize_mx(
                out=xcc[:, lo : lo + 2 * VOX].bitcast(FP8X4), scales=xcs[:, lo : lo + 2 * VOX], in_=gc[b][:]
            )

        def x_rmove(b):
            lo = 64 + 576 * b
            cs = xcI[:, lo : lo + VOX].rearrange("p (t c) -> p t c", c=64)
            ss = xsI[:, lo // 4 : lo // 4 + VOX // 4].rearrange("p (t c) -> p t c", c=16)
            nc.vector.tensor_copy(out=xrc4[:, b, 0, :, 8:64], in_=cs[:, :, 0:56])
            nc.vector.tensor_copy(out=xrs4[:, b, 0, :, 2:16], in_=ss[:, :, 0:14])
            nc.vector.tensor_copy(out=xrc4[:, b, 1, :, 0:56], in_=cs[:, :, 8:64])
            nc.vector.tensor_copy(out=xrs4[:, b, 1, :, 0:14], in_=ss[:, :, 2:16])

        def moving(b, k, c0, c1):
            if k < 3:
                lo = 576 * b + (64, 0, 128)[k]
                return xc[:, lo + c0 : lo + c1], xs[:, lo + c0 : lo + c1]
            lo = 2 * VOX * b + VOX * ((k - 3) % 2)
            if k < 5:
                return xrc[:, lo + c0 : lo + c1], xrs[:, lo + c0 : lo + c1]
            return xcc[:, lo + c0 : lo + c1], xcs[:, lo + c0 : lo + c1]

        banks = {}
        gws = {}

        def w_transpose(k, h):
            ps = bank(4 + 2 * (k % 2) + h)
            banks[(k, h)] = ps
            for kk in range(2):
                for u in range(2):
                    at = 256 * (2 * h + kk)
                    if k == SDIR:
                        words = wpm[:, at + 128 * u : at + 128 * u + 128]
                    else:
                        words = wrawF[:, 1024 * k + at + u : 1024 * k + at + 256 : 2]
                    nc.tensor.transpose(ps[:, 256 * kk + 128 * u : 256 * kk + 128 * u + 128], words, ident[:])

        def s_reorder():
            nc.scalar.copy(
                out=wpm[:].rearrange("p (m u q) -> p m u q", m=NM, u=2),
                in_=wrawF[:, 1024 * SDIR : 1024 * SDIR + 1024].rearrange("p (m q u) -> p m u q", m=NM, u=2),
            )

        def w_copy(k, h):
            if h == 0:
                gw = stage.tile([P, 1024], F32, name="gw", align_bytes=64)
                gws[k] = gw
            nc.scalar.copy(
                out=gws[k][:, 512 * h : 512 * h + 512].rearrange("p (k o u) -> p k o u", k=2, u=2),
                in_=banks[(k, h)][:].rearrange("p (k u o) -> p k o u", k=2, u=2),
            )

        def v_pick(k):
            i = VDIR.index(k)
            nc.scalar.copy(
                out=vin[i][:].rearrange("p (x h i) -> p x h i", x=16, h=2),
                in_=vraw[i][:].bitcast(F32).rearrange("p (x i h) -> p x h i", x=16, h=2),
            )

        def v_transpose(k):
            i = VDIR.index(k)
            nc.vector.transpose(out=vout[i][:], in_=vin[i][:])

        def v_copy(k):
            gw = stage.tile([P, 1024], F32, name="gw", align_bytes=64)
            gws[k] = gw
            dst = gw[:].rearrange("p (m x j h) -> p m x j h", m=NM, x=16, h=2)
            v = vout[VDIR.index(k)][:].rearrange("p (x h j m) -> p m x j h", x=16, h=2, m=NM)
            nc.scalar.copy(out=dst[:, 0:2], in_=v[:, 0:2])
            nc.vector.tensor_copy(out=dst[:, 2:4], in_=v[:, 2:4])

        def w_quant(k, h0, h1):
            lo = 512 * k
            nc.vector.quantize_mx(
                out=wc[:, lo + 256 * h0 : lo + 256 * h1].bitcast(FP8X4),
                scales=ws[:, lo + 256 * h0 : lo + 256 * h1],
                in_=gws[k][:, 512 * h0 : 512 * h1].bitcast(BF16),
            )

        def mx(acc, m, b, k, c0, c1):
            idx = 4 * k + m
            rc, rs = moving(b, k, c0, c1)
            nc.tensor.matmul_mx(
                out=acc[:, 0 : c1 - c0],
                lhsT=wc[:, P * idx : P * idx + P].bitcast(FP8X4),
                lhsT_scale=ws[:, P * idx : P * idx + P],
                rhs=rc.bitcast(FP8X4),
                rhs_scale=rs,
                start=(k == 0),
                stop=(k == NDIR - 1),
            )

        def copy_out(eng, dst, src):
            if eng == 0:
                nc.scalar.copy(out=dst, in_=src)
            else:
                nc.vector.tensor_copy(out=dst, in_=src)

        r_borders()
        c_borders(0)
        c_borders(1)

        def w_run(k):
            for h in range(2):
                w_transpose(k, h)
                w_copy(k, h)

        x_regroup(0, 0, 256)
        x_regroup(0, 256, 512)
        x_qself(0, 0, 256)
        x_qself(0, 256, 512)
        w_run(0)
        for h in range(2):
            dummy(1, xraw[0][:, 0:512])
            w_transpose(1, h)
            w_copy(1, h)
        w_quant(0, 0, 1)
        w_quant(0, 1, 2)
        x_rmove(0)
        acc0 = [bank(m) for m in range(NM)]

        def direction(k):
            for m in range(NM):
                mx(acc0[m], m, 0, k, 0, VOX)
                if k == NDIR - 1:
                    finish(acc0[m], 0, m, 0, VOX, m % 2)

        outs = [out[b].rearrange("(p m) t r c -> p m (t r c)", m=NM) for b in range(NB)]

        def finish(acc, b, m, c0, c1, eng):
            ob = ostage.tile([P, c1 - c0], F32, name="ob")
            copy_out(eng, ob[:], acc[:, 0 : c1 - c0])
            nc.sync.dma_start(out=outs[b][:, m, c0:c1], in_=ob[:])

        direction(0)
        w_quant(1, 0, 2)
        x_ccopy(0, nc.vector.tensor_copy)
        w_run(2)
        load_v(6, nc.scalar, (2, 3))
        direction(1)
        w_quant(2, 0, 2)
        x_regroup(1, 0, 512)
        w_run(3)
        direction(2)
        w_quant(3, 0, 2)
        x_qself(1, 0, 512)
        w_run(4)
        s_reorder()
        direction(3)
        w_quant(4, 0, 2)
        x_qc(0)

        acc1 = [bank(4 + m) for m in range(3)]

        def ahead(m, k0, k1):
            for k in range(k0, k1):
                mx(acc1[m], m, 1, k, 0, VOX)

        ahead(0, 0, 3)
        ahead(1, 0, 3)
        v_pick(6)
        w_run(5)
        x_rmove(1)
        v_transpose(6)
        direction(4)
        ahead(0, 3, 5)
        ahead(1, 3, 5)
        w_quant(5, 0, 2)
        direction(5)
        v_copy(6)
        w_quant(6, 0, 2)
        x_ccopy(1, nc.scalar.copy)
        x_qc(1)
        ahead(2, 0, 5)
        direction(6)

        for m in range(3):
            ahead(m, 5, NDIR)
            finish(acc1[m], 1, m, 0, VOX, (m + 1) % 2)
        for n, (i, c0, c1) in enumerate([(7, 0, VOX // 2), (0, VOX // 2, VOX)]):
            acc = bank(i)
            for k in range(NDIR):
                mx(acc, 3, 1, k, c0, c1)
            finish(acc, 1, 3, c0, c1, n % 2)
